import numpy as np
import ml_dtypes


def mxq(x, axis, fmt="e4m3"):
    dtype, down = {"e4m3": (ml_dtypes.float8_e4m3fn, 7), "e5m2": (ml_dtypes.float8_e5m2, 14)}[fmt]
    v = np.moveaxis(np.asarray(x, np.float32).astype(ml_dtypes.bfloat16).astype(np.float64), axis, -1)
    blocks = v.reshape(v.shape[:-1] + (-1, 32))
    amax = np.abs(blocks).max(-1, keepdims=True)
    byte = np.maximum(np.where(amax > 0, np.frexp(amax)[1] - 1 + 127, 0) - down, 1)
    scale = np.exp2(byte - 127.0)
    codes = (blocks / scale).astype(np.float32).astype(dtype).astype(np.float64)
    return np.moveaxis((codes * scale).reshape(v.shape), -1, axis)


WIDE = False


def mx_kscale(k):
    if not WIDE:
        return np.ones(k)
    levels = np.array([10, -10, 5, -5, 0])
    a = np.random.permutation(np.resize(levels, k // 512 * 4)).reshape(k // 512, 4)
    idx = np.arange(k)
    return np.exp2(a[idx // 512, idx % 128 // 32])


BF16 = ml_dtypes.bfloat16


def bf(x):
    return np.asarray(x, np.float32).astype(BF16)


def f64(x):
    return np.asarray(x).astype(np.float64)


E2M1 = np.array([0.0, 0.5, 1.0, 1.5, 2.0, 3.0, 4.0, 6.0, -0.0, -0.5, -1.0, -1.5, -2.0, -3.0, -4.0, -6.0])


def pack_weight(w, fmt):
    k, n = w.shape
    w = f64(bf(w)).reshape(k // 32, 32, n)
    amax = np.abs(w).max(1)
    if fmt == "e4m3":
        byte = np.frexp(amax)[1] - 1 + 127 - 7
    else:
        mant, ex = np.frexp(amax / 6.0)
        byte = np.where(mant > 0.5, ex, ex - 1) + 127
    byte = np.clip(np.where(amax > 0, byte, 1), 1, 254)
    scaled = (w * np.exp2(127.0 - byte)[:, None, :]).reshape(k, n).astype(np.float32)
    by_word = np.ascontiguousarray(scaled.reshape(k // 512, 128, 4, n).transpose(0, 1, 3, 2))
    if fmt == "e4m3":
        words = by_word.astype(ml_dtypes.float8_e4m3fn).view(np.uint8)
    else:
        c = by_word.astype(ml_dtypes.float4_e2m1fn).view(np.uint8) & 0xF
        words = c[..., 0::2] | (c[..., 1::2] << 4)
    return np.ascontiguousarray(words), np.ascontiguousarray(byte.astype(np.uint8).reshape(k // 512, 16, n))


def unpack_weight(words, scales, fmt):
    g, p, n, _ = words.shape
    if fmt == "e4m3":
        vals = np.ascontiguousarray(words).view(ml_dtypes.float8_e4m3fn).astype(np.float64)
    else:
        nib = np.empty((g, p, n, 4), np.uint8)
        nib[..., 0::2] = words & 0xF
        nib[..., 1::2] = words >> 4
        vals = E2M1[nib]
    vals = vals * np.repeat(np.exp2(scales.astype(np.float64) - 127.0), 8, axis=1)[..., None]
    return vals.transpose(0, 1, 3, 2).reshape(g * 512, n)


B, N, E, H, NOPE, VDIM, ROPE, QR, KVR = 4, 64, 512, 16, 64, 128, 64, 8192, 512
QH = NOPE + ROPE
BASE = 10000.0
FMT = "e4m3"


def rope(v):
    d = v.shape[-1]
    n = v.shape[-2]
    theta = BASE ** (-2.0 * np.arange(d // 2) / d)
    ang = np.arange(n)[:, None] * theta[None, :]
    cos, sin = np.cos(ang), np.sin(ang)
    v1, v2 = v[..., 0::2], v[..., 1::2]
    return np.stack([v1 * cos - v2 * sin, v1 * sin + v2 * cos], axis=-1).reshape(v.shape)


def setup_inputs():
    s, t = mx_kscale(E), mx_kscale(QR)
    x = bf(np.random.standard_normal((B, N, E)) * s)
    Wqa_words, Wqa_scales = pack_weight(np.random.standard_normal((E, QR)) / np.sqrt(E) / s[:, None] * t, FMT)
    Wqb_words, Wqb_scales = pack_weight(np.random.standard_normal((QR, H * QH)) / np.sqrt(QR) / t[:, None], FMT)
    return {"x": x,
            "Wqa_words": Wqa_words, "Wqa_scales": Wqa_scales,
            "Wqb_words": Wqb_words, "Wqb_scales": Wqb_scales}


def reference(x, Wqa_words, Wqa_scales, Wqb_words, Wqb_scales):
    cq = mxq(f64(x), 2, "e4m3") @ unpack_weight(Wqa_words, Wqa_scales, FMT)
    q = mxq(cq, 2, "e4m3") @ unpack_weight(Wqb_words, Wqb_scales, FMT)
    q = q.reshape(B, N, H, QH).transpose(0, 2, 1, 3)
    return np.concatenate([q[..., :NOPE], rope(q[..., NOPE:])], axis=-1)

@@ -1,0 +1,317 @@
+import math
+from contextlib import ExitStack
+
+import concourse.mybir as mybir
+from concourse.masks import make_identity
+
+F32 = mybir.dt.float32
+BF16 = mybir.dt.bfloat16
+I32 = mybir.dt.int32
+U32 = mybir.dt.uint32
+U8 = mybir.dt.uint8
+FP8X4 = mybir.dt.float8_e4m3fn_x4
+ALU = mybir.AluOpType
+ACT = mybir.ActivationFunctionType
+
+P = 128
+K_PASS = 512
+BANK_COLS = 512
+
+BATCH, POSITIONS, FEATURES = 4, 64, 512
+TOKEN_TILES = BATCH * POSITIONS // P
+TOKENS = TOKEN_TILES * P
+INNER = 8192
+GROUPS = INNER // K_PASS
+HEADS, HEAD_DIM, NOPE = 16, 128, 64
+PAIRS = (HEAD_DIM - NOPE) // 2
+ROPE_BASE = 10000.0
+Q_COLS = HEADS * HEAD_DIM
+HEADS_PER_BANK = BANK_COLS // HEAD_DIM
+HALF_COLS = Q_COLS // 2
+CHUNKS_PER_HALF = HALF_COLS // BANK_COLS
+
+PLANES_PER_TILE = 4
+QUADRANTS = 4
+WQA_PIECE_GROUPS = 2
+WQA_PIECES = GROUPS // WQA_PIECE_GROUPS
+WQA_PIECES_FIRST = 3
+LAG = 5
+TAIL_GROUPS = 4
+
+ROUND_TO_WHOLE = 1.5 * 2.0**23
+
+FLOPS = 2 * TOKENS * FEATURES * INNER + 2 * TOKENS * INNER * Q_COLS
+
+
+def tile_multilatentattention_pa_k_kernel(
+    tc, x, Wqa_words, Wqa_scales, Wqb_words, Wqb_scales, out
+):
+    nc = tc.nc
+    with ExitStack() as stack:
+        keep = stack.enter_context(tc.tile_pool(name="keep", bufs=1))
+        work = stack.enter_context(tc.tile_pool(name="work", bufs=3))
+        results = stack.enter_context(tc.tile_pool(name="results", bufs=4))
+        psum = stack.enter_context(tc.psum_pool(name="psum", bufs=1))
+        stack.enter_context(tc.manual_schedule())
+
+        def bank(index, name):
+            return psum.tile([P, BANK_COLS], F32, tag="bank%d" % index, name=name)
+
+        wqa_planes = keep.tile([P, INNER // PLANES_PER_TILE], U8, align_bytes=64)
+        nc.vector.memset(wqa_planes[:].bitcast(I32), 0)
+        wqb_planes = []
+        for s in range(GROUPS // PLANES_PER_TILE):
+            planes = keep.tile([P, Q_COLS], U8, name="wqb_planes%d" % s, align_bytes=64)
+            nc.vector.memset(planes[:].bitcast(I32), 0)
+            wqb_planes.append(planes)
+
+        wqa_words_dram = Wqa_words[0].rearrange("p n t -> p (n t)").bitcast(I32)
+        wqa_scales_dram = Wqa_scales[0].bitcast(I32)
+        wqb_words_dram = Wqb_words.rearrange("g p n t -> g p (n t)").bitcast(I32)
+        wqb_scales_dram = Wqb_scales.bitcast(I32)
+
+        x_rows = keep.tile([P, TOKEN_TILES, FEATURES], BF16)
+        for a in range(TOKEN_TILES):
+            nc.sync.dma_start(
+                out=x_rows[:, a, :], in_=x[2 * a : 2 * a + 2].rearrange("b n e -> n b e")
+            )
+
+        for quadrant in range(QUADRANTS):
+            nc.sync.dma_start(
+                out=wqa_planes[32 * quadrant : 32 * quadrant + 16, :].bitcast(I32),
+                in_=wqa_scales_dram[4 * quadrant : 4 * quadrant + 4, :].rearrange(
+                    "r (i n) -> i r n", i=PLANES_PER_TILE
+                ),
+            )
+
+        wqa_words = []
+
+        def load_wqa_piece():
+            piece = len(wqa_words)
+            width = WQA_PIECE_GROUPS * K_PASS
+            words = keep.tile([P, width], U32, name="wqa_words%d" % piece, align_bytes=64)
+            nc.sync.dma_start(
+                out=words[:].bitcast(I32),
+                in_=wqa_words_dram[:, piece * width : (piece + 1) * width],
+            )
+            wqa_words.append(words)
+
+        for piece in range(WQA_PIECES_FIRST):
+            load_wqa_piece()
+
+        for s in range(GROUPS // PLANES_PER_TILE):
+            for quadrant in range(QUADRANTS):
+                nc.sync.dma_start(
+                    out=wqb_planes[s][32 * quadrant : 32 * quadrant + 16, :].bitcast(I32),
+                    in_=wqb_scales_dram[
+                        PLANES_PER_TILE * s : PLANES_PER_TILE * (s + 1),
+                        4 * quadrant : 4 * quadrant + 4,
+                        :,
+                    ],
+                )
+
+        wqb_words = {}
+        for half in range(2):
+            for g in range(GROUPS):
+                words = keep.tile(
+                    [P, HALF_COLS], U32, name="wqb_words%d_%d" % (g, half), align_bytes=64
+                )
+                nc.sync.dma_start(
+                    out=words[:].bitcast(I32),
+                    in_=wqb_words_dram[g, :, half * HALF_COLS : (half + 1) * HALF_COLS],
+                )
+                wqb_words[(g, half)] = words
+                if g % WQA_PIECE_GROUPS == 0 and len(wqa_words) < WQA_PIECES:
+                    load_wqa_piece()
+
+        partition_index = keep.tile([P, 1], I32)
+        nc.gpsimd.iota(partition_index[:], pattern=[[0, 1]], base=0, channel_multiplier=1)
+        identity = keep.tile([P, P], F32)
+        make_identity(nc, identity[:])
+
+        position_int = keep.tile([P, 1], I32)
+        nc.vector.tensor_single_scalar(
+            out=position_int[:], in_=partition_index[:], scalar=1, op=ALU.arith_shift_right
+        )
+        position = keep.tile([P, 1], F32)
+        nc.vector.tensor_copy(out=position[:], in_=position_int[:])
+        turns = keep.tile([P, PAIRS], F32)
+        nc.vector.tensor_single_scalar(
+            out=turns[:, 0:1], in_=position[:], scalar=1.0 / (2.0 * math.pi), op=ALU.mult
+        )
+        width = 1
+        while width < PAIRS:
+            nc.vector.tensor_single_scalar(
+                out=turns[:, width : 2 * width],
+                in_=turns[:, 0:width],
+                scalar=ROPE_BASE ** (-width / PAIRS),
+                op=ALU.mult,
+            )
+            width *= 2
+        COS, SIN = 0, 1
+        shifted = keep.tile([P, 2, PAIRS], F32)
+        nc.vector.tensor_single_scalar(out=shifted[:, COS, :], in_=turns[:], scalar=0.25, op=ALU.add)
+        nc.vector.tensor_copy(out=shifted[:, SIN, :], in_=turns[:])
+        whole = keep.tile([P, 2, PAIRS], F32)
+        nc.vector.tensor_scalar(
+            out=whole[:],
+            in0=shifted[:],
+            scalar1=ROUND_TO_WHOLE,
+            scalar2=ROUND_TO_WHOLE,
+            op0=ALU.add,
+            op1=ALU.subtract,
+        )
+        part_turn = keep.tile([P, 2, PAIRS], F32)
+        nc.vector.tensor_tensor(out=part_turn[:], in0=shifted[:], in1=whole[:], op=ALU.subtract)
+        for_even = keep.tile([P, 2, PAIRS], F32)
+        for_odd = keep.tile([P, 2, PAIRS], F32)
+        nc.scalar.activation(out=for_even[:], in_=part_turn[:], func=ACT.Sin, scale=2.0 * math.pi)
+        nc.scalar.activation(
+            out=for_odd[:, 0, :], in_=part_turn[:, SIN, :], func=ACT.Sin, scale=-2.0 * math.pi
+        )
+        nc.scalar.activation(
+            out=for_odd[:, 1, :], in_=part_turn[:, COS, :], func=ACT.Sin, scale=2.0 * math.pi
+        )
+
+        def regroup(flipped, name):
+            grouped = work.tile([P, TOKENS * 4], BF16, tag="grouped", name=name, align_bytes=64)
+            nc.vector.tensor_copy(
+                out=grouped[:].bitcast(F32).rearrange("p (a r u) -> p a r u", a=TOKEN_TILES, u=2),
+                in_=flipped[:].rearrange("p (a u r) -> p a r u", a=TOKEN_TILES, u=2),
+            )
+            return grouped
+
+        def quantise(grouped, name):
+            codes = keep.tile([P, TOKENS], U32, name=name + "_codes", align_bytes=64)
+            scales = keep.tile([P, TOKENS], U8, name=name + "_scales", align_bytes=64)
+            nc.vector.quantize_mx(out=codes[:].bitcast(FP8X4), scales=scales[:], in_=grouped[:])
+            return codes, scales
+
+        x_flipped = bank(6, "x_flipped")
+        for a in range(TOKEN_TILES):
+            x_pairs = x_rows[:, a, :].bitcast(F32)
+            for u in range(2):
+                nc.tensor.transpose(
+                    x_flipped[:, (2 * a + u) * P : (2 * a + u + 1) * P],
+                    x_pairs[:, u : FEATURES // 2 : 2],
+                    identity[:],
+                )
+        x_codes, x_scales = quantise(regroup(x_flipped, "x_grouped"), "x")
+
+        cq_rows = {}
+        cq_grouped = {}
+        cq_codes = {}
+
+        def project(g):
+            piece, place = divmod(g, WQA_PIECE_GROUPS)
+            plane, plane_place = divmod(g, GROUPS // PLANES_PER_TILE)
+            rows = work.tile([P, TOKEN_TILES, K_PASS], BF16, tag="cq_rows", name="cq_rows%d" % g)
+            for a in range(TOKEN_TILES):
+                cq_bank = bank(4 + a, "cq_bank%d_%d" % (g, a))
+                nc.tensor.matmul_mx(
+                    out=cq_bank[:],
+                    lhsT=x_codes[:, a * P : (a + 1) * P].bitcast(FP8X4),
+                    lhsT_scale=x_scales[:, a * P : (a + 1) * P],
+                    rhs=wqa_words[piece][:, place * K_PASS : (place + 1) * K_PASS].bitcast(FP8X4),
+                    rhs_scale=wqa_planes[
+                        4 * plane : P, plane_place * K_PASS : (plane_place + 1) * K_PASS
+                    ],
+                    start=True,
+                    stop=True,
+                )
+                nc.scalar.copy(
+                    out=rows[:, a, :].rearrange("r (u p e) -> r u p e", u=2, e=2),
+                    in_=cq_bank[:].rearrange("r (p u e) -> r u p e", u=2, e=2),
+                )
+            cq_rows[g] = rows
+
+        def flip(g):
+            flipped = bank(6 + g % 2, "cq_flipped%d" % g)
+            for a in range(TOKEN_TILES):
+                pairs = cq_rows[g][:, a, :].bitcast(F32)
+                for u in range(2):
+                    nc.tensor.transpose(
+                        flipped[:, (2 * a + u) * P : (2 * a + u + 1) * P],
+                        pairs[:, u * P : (u + 1) * P],
+                        identity[:],
+                    )
+            cq_grouped[g] = regroup(flipped, "cq_grouped%d" % g)
+
+        def pack(g):
+            cq_codes[g] = quantise(cq_grouped[g], "cq%d" % g)
+
+        def accumulate(acc, g, a, chunk):
+            codes, scales = cq_codes[g]
+            half, place = divmod(chunk, CHUNKS_PER_HALF)
+            s, plane = divmod(g, PLANES_PER_TILE)
+            nc.tensor.matmul_mx(
+                out=acc[:],
+                lhsT=codes[:, a * P : (a + 1) * P].bitcast(FP8X4),
+                lhsT_scale=scales[:, a * P : (a + 1) * P],
+                rhs=wqb_words[(g, half)][:, place * BANK_COLS : (place + 1) * BANK_COLS].bitcast(FP8X4),
+                rhs_scale=wqb_planes[s][4 * plane : P, chunk * BANK_COLS : (chunk + 1) * BANK_COLS],
+                start=(g == 0),
+                stop=(g == GROUPS - 1),
+            )
+
+        def finish(acc, a, chunk):
+            heads = results.tile([P, HEADS_PER_BANK, HEAD_DIM], F32, tag="heads", name="heads%d_%d" % (a, chunk))
+            nc.scalar.copy(out=heads[:].rearrange("r h d -> r (h d)"), in_=acc[:])
+            pairs = heads[:, :, NOPE:HEAD_DIM].rearrange("r h (i e) -> r h i e", e=2)
+            shape = [P, HEADS_PER_BANK, 2, PAIRS]
+            from_even = results.tile(shape, F32, tag="from_even", name="from_even%d_%d" % (a, chunk))
+            from_odd = results.tile(shape, F32, tag="from_odd", name="from_odd%d_%d" % (a, chunk))
+            nc.vector.tensor_tensor(
+                out=from_even[:],
+                in0=pairs[:, :, :, 0].unsqueeze(2).to_broadcast(shape),
+                in1=for_even[:].unsqueeze(1).to_broadcast(shape),
+                op=ALU.mult,
+            )
+            nc.vector.tensor_tensor(
+                out=from_odd[:],
+                in0=pairs[:, :, :, 1].unsqueeze(2).to_broadcast(shape),
+                in1=for_odd[:].unsqueeze(1).to_broadcast(shape),
+                op=ALU.mult,
+            )
+            nc.vector.tensor_tensor(
+                out=pairs,
+                in0=from_even[:].rearrange("r h e i -> r h i e"),
+                in1=from_odd[:].rearrange("r h e i -> r h i e"),
+                op=ALU.add,
+            )
+            for h in range(HEADS_PER_BANK):
+                nc.sync.dma_start(
+                    out=out[2 * a : 2 * a + 2, HEADS_PER_BANK * chunk + h].rearrange("b n d -> n b d"),
+                    in_=heads[:, h, :],
+                )
+
+        def open_round(half, first_bank):
+            accs = []
+            for a in range(TOKEN_TILES):
+                for place in range(CHUNKS_PER_HALF):
+                    chunk = half * CHUNKS_PER_HALF + place
+                    accs.append((bank(first_bank + len(accs), "acc%d_%d" % (a, chunk)), a, chunk))
+            return accs
+
+        first_round = open_round(0, 0)
+        for step in range(GROUPS + LAG):
+            if step >= LAG:
+                for acc, a, chunk in first_round:
+                    accumulate(acc, step - LAG, a, chunk)
+            if step < GROUPS:
+                project(step)
+            if 1 <= step <= GROUPS:
+                flip(step - 1)
+            if 2 <= step <= GROUPS + 1:
+                pack(step - 2)
+        for acc, a, chunk in first_round:
+            finish(acc, a, chunk)
+
+        second_round = open_round(1, 4)
+        for g in range(GROUPS - TAIL_GROUPS):
+            for acc, a, chunk in second_round:
+                accumulate(acc, g, a, chunk)
+        for acc, a, chunk in second_round:
+            for g in range(GROUPS - TAIL_GROUPS, GROUPS):
+                accumulate(acc, g, a, chunk)
+            finish(acc, a, chunk)

@@ -34,8 +34,8 @@ PLANES_PER_TILE = 4
 QUADRANTS = 4
 WQA_PIECE_GROUPS = 2
 WQA_PIECES = GROUPS // WQA_PIECE_GROUPS
-WQA_PIECES_FIRST = 3
-LAG = 5
+WQA_PIECES_FIRST = 2
+LAG = 4
 TAIL_GROUPS = 4
 
 ROUND_TO_WHOLE = 1.5 * 2.0**23
@@ -65,10 +65,15 @@ def tile_multilatentattention_pa_k_kernel(
             nc.vector.memset(planes[:].bitcast(I32), 0)
             wqb_planes.append(planes)
 
+        partition_index = keep.tile([P, 1], I32)
+        nc.gpsimd.iota(partition_index[:], pattern=[[0, 1]], base=0, channel_multiplier=1)
+        identity = keep.tile([P, P], F32)
+        make_identity(nc, identity[:])
+
         wqa_words_dram = Wqa_words[0].rearrange("p n t -> p (n t)").bitcast(I32)
         wqa_scales_dram = Wqa_scales[0].bitcast(I32)
         wqb_words_dram = Wqb_words.rearrange("g p n t -> g p (n t)").bitcast(I32)
-        wqb_scales_dram = Wqb_scales.bitcast(I32)
+        wqb_scales_dram = Wqb_scales.bitcast(F32)
 
         x_rows = keep.tile([P, TOKEN_TILES, FEATURES], BF16)
         for a in range(TOKEN_TILES):
@@ -101,8 +106,8 @@ def tile_multilatentattention_pa_k_kernel(
 
         for s in range(GROUPS // PLANES_PER_TILE):
             for quadrant in range(QUADRANTS):
-                nc.sync.dma_start(
-                    out=wqb_planes[s][32 * quadrant : 32 * quadrant + 16, :].bitcast(I32),
+                nc.gpsimd.dma_start(
+                    out=wqb_planes[s][32 * quadrant : 32 * quadrant + 16, :].bitcast(F32),
                     in_=wqb_scales_dram[
                         PLANES_PER_TILE * s : PLANES_PER_TILE * (s + 1),
                         4 * quadrant : 4 * quadrant + 4,
@@ -121,13 +126,8 @@ def tile_multilatentattention_pa_k_kernel(
                     in_=wqb_words_dram[g, :, half * HALF_COLS : (half + 1) * HALF_COLS],
                 )
                 wqb_words[(g, half)] = words
-                if g % WQA_PIECE_GROUPS == 0 and len(wqa_words) < WQA_PIECES:
+                if g % WQA_PIECE_GROUPS == WQA_PIECE_GROUPS - 1 and len(wqa_words) < WQA_PIECES:
                     load_wqa_piece()
-
-        partition_index = keep.tile([P, 1], I32)
-        nc.gpsimd.iota(partition_index[:], pattern=[[0, 1]], base=0, channel_multiplier=1)
-        identity = keep.tile([P, P], F32)
-        make_identity(nc, identity[:])
 
         position_int = keep.tile([P, 1], I32)
         nc.vector.tensor_single_scalar(

@@ -14,7 +14,8 @@ ALU = mybir.AluOpType
 ACT = mybir.ActivationFunctionType
 
 P = 128
-K_PASS = 512
+PACK = 4
+K_PASS = P * PACK
 BANK_COLS = 512
 
 BATCH, POSITIONS, FEATURES = 4, 64, 512
@@ -32,11 +33,9 @@ CHUNKS_PER_HALF = HALF_COLS // BANK_COLS
 
 PLANES_PER_TILE = 4
 QUADRANTS = 4
-WQA_PIECE_GROUPS = 2
-WQA_PIECES = GROUPS // WQA_PIECE_GROUPS
-WQA_PIECES_FIRST = 2
+STEP_GROUPS = 2
 LAG = 4
-TAIL_GROUPS = 4
+TAIL_GROUPS = 5
 
 ROUND_TO_WHOLE = 1.5 * 2.0**23
 
@@ -49,7 +48,7 @@ def tile_multilatentattention_pa_k_kernel(
     nc = tc.nc
     with ExitStack() as stack:
         keep = stack.enter_context(tc.tile_pool(name="keep", bufs=1))
-        work = stack.enter_context(tc.tile_pool(name="work", bufs=3))
+        work = stack.enter_context(tc.tile_pool(name="work", bufs=2 * STEP_GROUPS))
         results = stack.enter_context(tc.tile_pool(name="results", bufs=4))
         psum = stack.enter_context(tc.psum_pool(name="psum", bufs=1))
         stack.enter_context(tc.manual_schedule())
@@ -65,21 +64,21 @@ def tile_multilatentattention_pa_k_kernel(
             nc.vector.memset(planes[:].bitcast(I32), 0)
             wqb_planes.append(planes)
 
-        partition_index = keep.tile([P, 1], I32)
-        nc.gpsimd.iota(partition_index[:], pattern=[[0, 1]], base=0, channel_multiplier=1)
         identity = keep.tile([P, P], F32)
         make_identity(nc, identity[:])
+        partition_index = keep.tile([P, 1], I32)
+        nc.gpsimd.iota(partition_index[:], pattern=[[0, 1]], base=0, channel_multiplier=1)
 
         wqa_words_dram = Wqa_words[0].rearrange("p n t -> p (n t)").bitcast(I32)
         wqa_scales_dram = Wqa_scales[0].bitcast(I32)
         wqb_words_dram = Wqb_words.rearrange("g p n t -> g p (n t)").bitcast(I32)
         wqb_scales_dram = Wqb_scales.bitcast(F32)
 
-        x_rows = keep.tile([P, TOKEN_TILES, FEATURES], BF16)
+        x_rows = []
         for a in range(TOKEN_TILES):
-            nc.sync.dma_start(
-                out=x_rows[:, a, :], in_=x[2 * a : 2 * a + 2].rearrange("b n e -> n b e")
-            )
+            rows = keep.tile([P, FEATURES], BF16, name="x_rows%d" % a)
+            nc.sync.dma_start(out=rows[:], in_=x[2 * a : 2 * a + 2].rearrange("b n e -> n b e"))
+            x_rows.append(rows)
 
         for quadrant in range(QUADRANTS):
             nc.sync.dma_start(
@@ -88,21 +87,6 @@ def tile_multilatentattention_pa_k_kernel(
                     "r (i n) -> i r n", i=PLANES_PER_TILE
                 ),
             )
-
-        wqa_words = []
-
-        def load_wqa_piece():
-            piece = len(wqa_words)
-            width = WQA_PIECE_GROUPS * K_PASS
-            words = keep.tile([P, width], U32, name="wqa_words%d" % piece, align_bytes=64)
-            nc.sync.dma_start(
-                out=words[:].bitcast(I32),
-                in_=wqa_words_dram[:, piece * width : (piece + 1) * width],
-            )
-            wqa_words.append(words)
-
-        for piece in range(WQA_PIECES_FIRST):
-            load_wqa_piece()
 
         for s in range(GROUPS // PLANES_PER_TILE):
             for quadrant in range(QUADRANTS):
@@ -115,6 +99,18 @@ def tile_multilatentattention_pa_k_kernel(
                     ],
                 )
 
+        wqa_words = []
+
+        def load_wqa_group():
+            g = len(wqa_words)
+            words = keep.tile([P, K_PASS], U32, name="wqa_words%d" % g, align_bytes=64)
+            nc.sync.dma_start(
+                out=words[:].bitcast(I32), in_=wqa_words_dram[:, g * K_PASS : (g + 1) * K_PASS]
+            )
+            wqa_words.append(words)
+
+        for g in range(LAG):
+            load_wqa_group()
         wqb_words = {}
         for half in range(2):
             for g in range(GROUPS):
@@ -126,8 +122,117 @@ def tile_multilatentattention_pa_k_kernel(
                     in_=wqb_words_dram[g, :, half * HALF_COLS : (half + 1) * HALF_COLS],
                 )
                 wqb_words[(g, half)] = words
-                if g % WQA_PIECE_GROUPS == WQA_PIECE_GROUPS - 1 and len(wqa_words) < WQA_PIECES:
-                    load_wqa_piece()
+                if len(wqa_words) < GROUPS:
+                    load_wqa_group()
+
+        def regroup(grouped, flipped):
+            nc.vector.tensor_copy(
+                out=grouped.bitcast(F32).rearrange("p (a r u) -> p a r u", r=P, u=2),
+                in_=flipped.rearrange("p (a u r) -> p a r u", r=P, u=2),
+            )
+
+        x_grouped = keep.tile([P, TOKENS * PACK], BF16, align_bytes=64)
+        x_codes = keep.tile([P, TOKENS], U32, align_bytes=64)
+        x_scales = keep.tile([P, TOKENS], U8, align_bytes=64)
+        for a in range(TOKEN_TILES):
+            x_flipped = bank(6 + a, "x_flipped%d" % a)
+            x_pairs = x_rows[a][:].bitcast(F32)
+            for u in range(2):
+                nc.tensor.transpose(
+                    x_flipped[:, u * P : (u + 1) * P], x_pairs[:, u : FEATURES // 2 : 2], identity[:]
+                )
+            regroup(x_grouped[:, a * K_PASS : (a + 1) * K_PASS], x_flipped[:, 0 : 2 * P])
+            nc.vector.quantize_mx(
+                out=x_codes[:, a * P : (a + 1) * P].bitcast(FP8X4),
+                scales=x_scales[:, a * P : (a + 1) * P],
+                in_=x_grouped[:, a * K_PASS : (a + 1) * K_PASS],
+            )
+
+        cq_rows = {}
+        cq_grouped = {}
+        cq_codes = {}
+
+        def project(g):
+            plane, place = divmod(g, GROUPS // PLANES_PER_TILE)
+            rows = work.tile([P, TOKEN_TILES, K_PASS], BF16, tag="cq_rows", name="cq_rows%d" % g)
+            for a in range(TOKEN_TILES):
+                cq_bank = bank(4 + a, "cq_bank%d_%d" % (g, a))
+                nc.tensor.matmul_mx(
+                    out=cq_bank[:],
+                    lhsT=x_codes[:, a * P : (a + 1) * P].bitcast(FP8X4),
+                    lhsT_scale=x_scales[:, a * P : (a + 1) * P],
+                    rhs=wqa_words[g][:].bitcast(FP8X4),
+                    rhs_scale=wqa_planes[4 * plane : P, place * K_PASS : (place + 1) * K_PASS],
+                    start=True,
+                    stop=True,
+                )
+                nc.scalar.copy(
+                    out=rows[:, a, :].rearrange("r (u p e) -> r u p e", u=2, e=2),
+                    in_=cq_bank[:].rearrange("r (p u e) -> r u p e", u=2, e=2),
+                )
+            cq_rows[g] = rows
+
+        def flip(g):
+            flipped = bank(6 + g % STEP_GROUPS, "cq_flipped%d" % g)
+            for a in range(TOKEN_TILES):
+                pairs = cq_rows[g][:, a, :].bitcast(F32)
+                for u in range(2):
+                    nc.tensor.transpose(
+                        flipped[:, (2 * a + u) * P : (2 * a + u + 1) * P],
+                        pairs[:, u * P : (u + 1) * P],
+                        identity[:],
+                    )
+            grouped = work.tile(
+                [P, TOKENS * PACK], BF16, tag="cq_grouped", name="cq_grouped%d" % g, align_bytes=64
+            )
+            regroup(grouped[:], flipped[:])
+            cq_grouped[g] = grouped
+
+        def pack(g):
+            codes = keep.tile([P, TOKENS], U32, name="cq_codes%d" % g, align_bytes=64)
+            scales = keep.tile([P, TOKENS], U8, name="cq_scales%d" % g, align_bytes=64)
+            nc.vector.quantize_mx(
+                out=codes[:].bitcast(FP8X4), scales=scales[:], in_=cq_grouped[g][:]
+            )
+            cq_codes[g] = (codes, scales)
+
+        def accumulate(acc, g, a, chunk):
+            codes, scales = cq_codes[g]
+            half, place = divmod(chunk, CHUNKS_PER_HALF)
+            s, plane = divmod(g, PLANES_PER_TILE)
+            nc.tensor.matmul_mx(
+                out=acc[:],
+                lhsT=codes[:, a * P : (a + 1) * P].bitcast(FP8X4),
+                lhsT_scale=scales[:, a * P : (a + 1) * P],
+                rhs=wqb_words[(g, half)][:, place * BANK_COLS : (place + 1) * BANK_COLS].bitcast(FP8X4),
+                rhs_scale=wqb_planes[s][4 * plane : P, chunk * BANK_COLS : (chunk + 1) * BANK_COLS],
+                start=(g == 0),
+                stop=(g == GROUPS - 1),
+            )
+
+        def open_round(half, first_bank):
+            accs = []
+            for a in range(TOKEN_TILES):
+                for place in range(CHUNKS_PER_HALF):
+                    chunk = half * CHUNKS_PER_HALF + place
+                    accs.append((bank(first_bank + len(accs), "acc%d_%d" % (a, chunk)), a, chunk))
+            return accs
+
+        first_round = open_round(0, 0)
+        for first in range(0, GROUPS + LAG, STEP_GROUPS):
+            if first < GROUPS:
+                project(first)
+            made_before = [g for g in range(first - STEP_GROUPS, first) if 0 <= g < GROUPS]
+            for g in made_before:
+                flip(g)
+            for g in made_before:
+                pack(g)
+            if first + 1 < GROUPS:
+                project(first + 1)
+            for g in range(first - LAG, first - LAG + STEP_GROUPS):
+                if g >= 0:
+                    for acc, a, chunk in first_round:
+                        accumulate(acc, g, a, chunk)
 
         position_int = keep.tile([P, 1], I32)
         nc.vector.tensor_single_scalar(
@@ -173,94 +278,15 @@ def tile_multilatentattention_pa_k_kernel(
             out=for_odd[:, 1, :], in_=part_turn[:, COS, :], func=ACT.Sin, scale=2.0 * math.pi
         )
 
-        def regroup(flipped, name):
-            grouped = work.tile([P, TOKENS * 4], BF16, tag="grouped", name=name, align_bytes=64)
-            nc.vector.tensor_copy(
-                out=grouped[:].bitcast(F32).rearrange("p (a r u) -> p a r u", a=TOKEN_TILES, u=2),
-                in_=flipped[:].rearrange("p (a u r) -> p a r u", a=TOKEN_TILES, u=2),
-            )
-            return grouped
-
-        def quantise(grouped, name):
-            codes = keep.tile([P, TOKENS], U32, name=name + "_codes", align_bytes=64)
-            scales = keep.tile([P, TOKENS], U8, name=name + "_scales", align_bytes=64)
-            nc.vector.quantize_mx(out=codes[:].bitcast(FP8X4), scales=scales[:], in_=grouped[:])
-            return codes, scales
-
-        x_flipped = bank(6, "x_flipped")
-        for a in range(TOKEN_TILES):
-            x_pairs = x_rows[:, a, :].bitcast(F32)
-            for u in range(2):
-                nc.tensor.transpose(
-                    x_flipped[:, (2 * a + u) * P : (2 * a + u + 1) * P],
-                    x_pairs[:, u : FEATURES // 2 : 2],
-                    identity[:],
-                )
-        x_codes, x_scales = quantise(regroup(x_flipped, "x_grouped"), "x")
-
-        cq_rows = {}
-        cq_grouped = {}
-        cq_codes = {}
-
-        def project(g):
-            piece, place = divmod(g, WQA_PIECE_GROUPS)
-            plane, plane_place = divmod(g, GROUPS // PLANES_PER_TILE)
-            rows = work.tile([P, TOKEN_TILES, K_PASS], BF16, tag="cq_rows", name="cq_rows%d" % g)
-            for a in range(TOKEN_TILES):
-                cq_bank = bank(4 + a, "cq_bank%d_%d" % (g, a))
-                nc.tensor.matmul_mx(
-                    out=cq_bank[:],
-                    lhsT=x_codes[:, a * P : (a + 1) * P].bitcast(FP8X4),
-                    lhsT_scale=x_scales[:, a * P : (a + 1) * P],
-                    rhs=wqa_words[piece][:, place * K_PASS : (place + 1) * K_PASS].bitcast(FP8X4),
-                    rhs_scale=wqa_planes[
-                        4 * plane : P, plane_place * K_PASS : (plane_place + 1) * K_PASS
-                    ],
-                    start=True,
-                    stop=True,
-                )
-                nc.scalar.copy(
-                    out=rows[:, a, :].rearrange("r (u p e) -> r u p e", u=2, e=2),
-                    in_=cq_bank[:].rearrange("r (p u e) -> r u p e", u=2, e=2),
-                )
-            cq_rows[g] = rows
-
-        def flip(g):
-            flipped = bank(6 + g % 2, "cq_flipped%d" % g)
-            for a in range(TOKEN_TILES):
-                pairs = cq_rows[g][:, a, :].bitcast(F32)
-                for u in range(2):
-                    nc.tensor.transpose(
-                        flipped[:, (2 * a + u) * P : (2 * a + u + 1) * P],
-                        pairs[:, u * P : (u + 1) * P],
-                        identity[:],
-                    )
-            cq_grouped[g] = regroup(flipped, "cq_grouped%d" % g)
-
-        def pack(g):
-            cq_codes[g] = quantise(cq_grouped[g], "cq%d" % g)
-
-        def accumulate(acc, g, a, chunk):
-            codes, scales = cq_codes[g]
-            half, place = divmod(chunk, CHUNKS_PER_HALF)
-            s, plane = divmod(g, PLANES_PER_TILE)
-            nc.tensor.matmul_mx(
-                out=acc[:],
-                lhsT=codes[:, a * P : (a + 1) * P].bitcast(FP8X4),
-                lhsT_scale=scales[:, a * P : (a + 1) * P],
-                rhs=wqb_words[(g, half)][:, place * BANK_COLS : (place + 1) * BANK_COLS].bitcast(FP8X4),
-                rhs_scale=wqb_planes[s][4 * plane : P, chunk * BANK_COLS : (chunk + 1) * BANK_COLS],
-                start=(g == 0),
-                stop=(g == GROUPS - 1),
-            )
-
         def finish(acc, a, chunk):
-            heads = results.tile([P, HEADS_PER_BANK, HEAD_DIM], F32, tag="heads", name="heads%d_%d" % (a, chunk))
-            nc.scalar.copy(out=heads[:].rearrange("r h d -> r (h d)"), in_=acc[:])
-            pairs = heads[:, :, NOPE:HEAD_DIM].rearrange("r h (i e) -> r h i e", e=2)
+            label = "%d_%d" % (a, chunk)
+            summed = acc[:].rearrange("r (h d) -> r h d", h=HEADS_PER_BANK)
+            heads = results.tile([P, HEADS_PER_BANK, HEAD_DIM], F32, tag="heads", name="heads" + label)
+            nc.scalar.copy(out=heads[:, :, 0:NOPE], in_=summed[:, :, 0:NOPE])
+            pairs = summed[:, :, NOPE:HEAD_DIM].rearrange("r h (i e) -> r h i e", e=2)
             shape = [P, HEADS_PER_BANK, 2, PAIRS]
-            from_even = results.tile(shape, F32, tag="from_even", name="from_even%d_%d" % (a, chunk))
-            from_odd = results.tile(shape, F32, tag="from_odd", name="from_odd%d_%d" % (a, chunk))
+            from_even = results.tile(shape, F32, tag="from_even", name="from_even" + label)
+            from_odd = results.tile(shape, F32, tag="from_odd", name="from_odd" + label)
             nc.vector.tensor_tensor(
                 out=from_even[:],
                 in0=pairs[:, :, :, 0].unsqueeze(2).to_broadcast(shape),
@@ -274,7 +300,7 @@ def tile_multilatentattention_pa_k_kernel(
                 op=ALU.mult,
             )
             nc.vector.tensor_tensor(
-                out=pairs,
+                out=heads[:, :, NOPE:HEAD_DIM].rearrange("r h (i e) -> r h i e", e=2),
                 in0=from_even[:].rearrange("r h e i -> r h i e"),
                 in1=from_odd[:].rearrange("r h e i -> r h i e"),
                 op=ALU.add,
@@ -285,25 +311,6 @@ def tile_multilatentattention_pa_k_kernel(
                     in_=heads[:, h, :],
                 )
 
-        def open_round(half, first_bank):
-            accs = []
-            for a in range(TOKEN_TILES):
-                for place in range(CHUNKS_PER_HALF):
-                    chunk = half * CHUNKS_PER_HALF + place
-                    accs.append((bank(first_bank + len(accs), "acc%d_%d" % (a, chunk)), a, chunk))
-            return accs
-
-        first_round = open_round(0, 0)
-        for step in range(GROUPS + LAG):
-            if step >= LAG:
-                for acc, a, chunk in first_round:
-                    accumulate(acc, step - LAG, a, chunk)
-            if step < GROUPS:
-                project(step)
-            if 1 <= step <= GROUPS:
-                flip(step - 1)
-            if 2 <= step <= GROUPS + 1:
-                pack(step - 2)
         for acc, a, chunk in first_round:
             finish(acc, a, chunk)
 

@@ -35,7 +35,7 @@ PLANES_PER_TILE = 4
 QUADRANTS = 4
 STEP_GROUPS = 2
 LAG = 4
-TAIL_GROUPS = 5
+TAIL_GROUPS = 4
 
 ROUND_TO_WHOLE = 1.5 * 2.0**23
 
@@ -112,18 +112,31 @@ def tile_multilatentattention_pa_k_kernel(
         for g in range(LAG):
             load_wqa_group()
         wqb_words = {}
-        for half in range(2):
-            for g in range(GROUPS):
-                words = keep.tile(
-                    [P, HALF_COLS], U32, name="wqb_words%d_%d" % (g, half), align_bytes=64
-                )
-                nc.sync.dma_start(
-                    out=words[:].bitcast(I32),
-                    in_=wqb_words_dram[g, :, half * HALF_COLS : (half + 1) * HALF_COLS],
-                )
-                wqb_words[(g, half)] = words
-                if len(wqa_words) < GROUPS:
-                    load_wqa_group()
+
+        def load_wqb(g, first_chunk, chunks):
+            words = keep.tile(
+                [P, chunks * BANK_COLS], U32, name="wqb_words%d_%d" % (g, first_chunk), align_bytes=64
+            )
+            nc.sync.dma_start(
+                out=words[:].bitcast(I32),
+                in_=wqb_words_dram[
+                    g, :, first_chunk * BANK_COLS : (first_chunk + chunks) * BANK_COLS
+                ],
+            )
+            for place in range(chunks):
+                wqb_words[(g, first_chunk + place)] = words[
+                    :, place * BANK_COLS : (place + 1) * BANK_COLS
+                ]
+
+        for g in range(GROUPS):
+            load_wqb(g, 0, CHUNKS_PER_HALF)
+            if len(wqa_words) < GROUPS:
+                load_wqa_group()
+        for g in range(GROUPS - TAIL_GROUPS):
+            load_wqb(g, CHUNKS_PER_HALF, CHUNKS_PER_HALF)
+        for chunk in range(CHUNKS_PER_HALF, 2 * CHUNKS_PER_HALF):
+            for g in range(GROUPS - TAIL_GROUPS, GROUPS):
+                load_wqb(g, chunk, 1)
 
         def regroup(grouped, flipped):
             nc.vector.tensor_copy(
@@ -152,30 +165,29 @@ def tile_multilatentattention_pa_k_kernel(
         cq_grouped = {}
         cq_codes = {}
 
-        def project(g):
+        def project(g, a):
             plane, place = divmod(g, GROUPS // PLANES_PER_TILE)
-            rows = work.tile([P, TOKEN_TILES, K_PASS], BF16, tag="cq_rows", name="cq_rows%d" % g)
-            for a in range(TOKEN_TILES):
-                cq_bank = bank(4 + a, "cq_bank%d_%d" % (g, a))
-                nc.tensor.matmul_mx(
-                    out=cq_bank[:],
-                    lhsT=x_codes[:, a * P : (a + 1) * P].bitcast(FP8X4),
-                    lhsT_scale=x_scales[:, a * P : (a + 1) * P],
-                    rhs=wqa_words[g][:].bitcast(FP8X4),
-                    rhs_scale=wqa_planes[4 * plane : P, place * K_PASS : (place + 1) * K_PASS],
-                    start=True,
-                    stop=True,
-                )
-                nc.scalar.copy(
-                    out=rows[:, a, :].rearrange("r (u p e) -> r u p e", u=2, e=2),
-                    in_=cq_bank[:].rearrange("r (p u e) -> r u p e", u=2, e=2),
-                )
-            cq_rows[g] = rows
+            cq_bank = bank(4 + a, "cq_bank%d_%d" % (g, a))
+            nc.tensor.matmul_mx(
+                out=cq_bank[:],
+                lhsT=x_codes[:, a * P : (a + 1) * P].bitcast(FP8X4),
+                lhsT_scale=x_scales[:, a * P : (a + 1) * P],
+                rhs=wqa_words[g][:].bitcast(FP8X4),
+                rhs_scale=wqa_planes[4 * plane : P, place * K_PASS : (place + 1) * K_PASS],
+                start=True,
+                stop=True,
+            )
+            rows = work.tile([P, K_PASS], BF16, tag="cq_rows%d" % a, name="cq_rows%d_%d" % (g, a))
+            nc.scalar.copy(
+                out=rows[:].rearrange("r (u p e) -> r u p e", u=2, e=2),
+                in_=cq_bank[:].rearrange("r (p u e) -> r u p e", u=2, e=2),
+            )
+            cq_rows[(g, a)] = rows
 
         def flip(g):
             flipped = bank(6 + g % STEP_GROUPS, "cq_flipped%d" % g)
             for a in range(TOKEN_TILES):
-                pairs = cq_rows[g][:, a, :].bitcast(F32)
+                pairs = cq_rows[(g, a)][:].bitcast(F32)
                 for u in range(2):
                     nc.tensor.transpose(
                         flipped[:, (2 * a + u) * P : (2 * a + u + 1) * P],
@@ -198,13 +210,12 @@ def tile_multilatentattention_pa_k_kernel(
 
         def accumulate(acc, g, a, chunk):
             codes, scales = cq_codes[g]
-            half, place = divmod(chunk, CHUNKS_PER_HALF)
             s, plane = divmod(g, PLANES_PER_TILE)
             nc.tensor.matmul_mx(
                 out=acc[:],
                 lhsT=codes[:, a * P : (a + 1) * P].bitcast(FP8X4),
                 lhsT_scale=scales[:, a * P : (a + 1) * P],
-                rhs=wqb_words[(g, half)][:, place * BANK_COLS : (place + 1) * BANK_COLS].bitcast(FP8X4),
+                rhs=wqb_words[(g, chunk)].bitcast(FP8X4),
                 rhs_scale=wqb_planes[s][4 * plane : P, chunk * BANK_COLS : (chunk + 1) * BANK_COLS],
                 start=(g == 0),
                 stop=(g == GROUPS - 1),
@@ -212,27 +223,30 @@ def tile_multilatentattention_pa_k_kernel(
 
         def open_round(half, first_bank):
             accs = []
-            for a in range(TOKEN_TILES):
-                for place in range(CHUNKS_PER_HALF):
-                    chunk = half * CHUNKS_PER_HALF + place
+            for chunk in range(half * CHUNKS_PER_HALF, (half + 1) * CHUNKS_PER_HALF):
+                for a in range(TOKEN_TILES):
                     accs.append((bank(first_bank + len(accs), "acc%d_%d" % (a, chunk)), a, chunk))
             return accs
 
         first_round = open_round(0, 0)
+
+        def advance(g):
+            for a in range(TOKEN_TILES):
+                if g < GROUPS:
+                    project(g, a)
+                if g >= LAG:
+                    for acc, acc_tile, chunk in first_round:
+                        if acc_tile == a:
+                            accumulate(acc, g - LAG, a, chunk)
+
         for first in range(0, GROUPS + LAG, STEP_GROUPS):
-            if first < GROUPS:
-                project(first)
+            advance(first)
             made_before = [g for g in range(first - STEP_GROUPS, first) if 0 <= g < GROUPS]
             for g in made_before:
                 flip(g)
             for g in made_before:
                 pack(g)
-            if first + 1 < GROUPS:
-                project(first + 1)
-            for g in range(first - LAG, first - LAG + STEP_GROUPS):
-                if g >= 0:
-                    for acc, a, chunk in first_round:
-                        accumulate(acc, g, a, chunk)
+            advance(first + 1)
 
         position_int = keep.tile([P, 1], I32)
         nc.vector.tensor_single_scalar(

@@ -33,8 +33,9 @@ CHUNKS_PER_HALF = HALF_COLS // BANK_COLS
 
 PLANES_PER_TILE = 4
 QUADRANTS = 4
-STEP_GROUPS = 2
 LAG = 4
+PLANE_GROUPS = GROUPS // PLANES_PER_TILE
+ORDER = [place + PLANE_GROUPS * plane for place in range(PLANE_GROUPS) for plane in range(PLANES_PER_TILE)]
 TAIL_GROUPS = 4
 
 ROUND_TO_WHOLE = 1.5 * 2.0**23
@@ -48,7 +49,7 @@ def tile_multilatentattention_pa_k_kernel(
     nc = tc.nc
     with ExitStack() as stack:
         keep = stack.enter_context(tc.tile_pool(name="keep", bufs=1))
-        work = stack.enter_context(tc.tile_pool(name="work", bufs=2 * STEP_GROUPS))
+        work = stack.enter_context(tc.tile_pool(name="work", bufs=4))
         results = stack.enter_context(tc.tile_pool(name="results", bufs=4))
         psum = stack.enter_context(tc.psum_pool(name="psum", bufs=1))
         stack.enter_context(tc.manual_schedule())
@@ -58,6 +59,7 @@ def tile_multilatentattention_pa_k_kernel(
 
         wqa_planes = keep.tile([P, INNER // PLANES_PER_TILE], U8, align_bytes=64)
         nc.vector.memset(wqa_planes[:].bitcast(I32), 0)
+        wqa_sorted_planes = keep.tile([P, INNER // PLANES_PER_TILE], U8, align_bytes=64)
         wqb_planes = []
         for s in range(GROUPS // PLANES_PER_TILE):
             planes = keep.tile([P, Q_COLS], U8, name="wqb_planes%d" % s, align_bytes=64)
@@ -93,23 +95,23 @@ def tile_multilatentattention_pa_k_kernel(
                 nc.gpsimd.dma_start(
                     out=wqb_planes[s][32 * quadrant : 32 * quadrant + 16, :].bitcast(F32),
                     in_=wqb_scales_dram[
-                        PLANES_PER_TILE * s : PLANES_PER_TILE * (s + 1),
+                        s : GROUPS : PLANE_GROUPS,
                         4 * quadrant : 4 * quadrant + 4,
                         :,
                     ],
                 )
 
-        wqa_words = []
+        wqa_words = {}
 
         def load_wqa_group():
-            g = len(wqa_words)
+            g = ORDER[len(wqa_words)]
             words = keep.tile([P, K_PASS], U32, name="wqa_words%d" % g, align_bytes=64)
             nc.sync.dma_start(
                 out=words[:].bitcast(I32), in_=wqa_words_dram[:, g * K_PASS : (g + 1) * K_PASS]
             )
-            wqa_words.append(words)
+            wqa_words[g] = words
 
-        for g in range(LAG):
+        for turn in range(LAG):
             load_wqa_group()
         wqb_words = {}
 
@@ -128,14 +130,14 @@ def tile_multilatentattention_pa_k_kernel(
                     :, place * BANK_COLS : (place + 1) * BANK_COLS
                 ]
 
-        for g in range(GROUPS):
+        for g in ORDER:
             load_wqb(g, 0, CHUNKS_PER_HALF)
             if len(wqa_words) < GROUPS:
                 load_wqa_group()
-        for g in range(GROUPS - TAIL_GROUPS):
+        for g in ORDER[:-TAIL_GROUPS]:
             load_wqb(g, CHUNKS_PER_HALF, CHUNKS_PER_HALF)
         for chunk in range(CHUNKS_PER_HALF, 2 * CHUNKS_PER_HALF):
-            for g in range(GROUPS - TAIL_GROUPS, GROUPS):
+            for g in ORDER[-TAIL_GROUPS:]:
                 load_wqb(g, chunk, 1)
 
         def regroup(grouped, flipped):
@@ -161,44 +163,50 @@ def tile_multilatentattention_pa_k_kernel(
                 in_=x_grouped[:, a * K_PASS : (a + 1) * K_PASS],
             )
 
-        cq_rows = {}
+        sorted_words = {}
         cq_grouped = {}
         cq_codes = {}
 
-        def project(g, a):
-            plane, place = divmod(g, GROUPS // PLANES_PER_TILE)
-            cq_bank = bank(4 + a, "cq_bank%d_%d" % (g, a))
-            nc.tensor.matmul_mx(
-                out=cq_bank[:],
-                lhsT=x_codes[:, a * P : (a + 1) * P].bitcast(FP8X4),
-                lhsT_scale=x_scales[:, a * P : (a + 1) * P],
-                rhs=wqa_words[g][:].bitcast(FP8X4),
-                rhs_scale=wqa_planes[4 * plane : P, place * K_PASS : (place + 1) * K_PASS],
-                start=True,
-                stop=True,
+        def sort_columns(sorted_, plain):
+            nc.vector.tensor_copy(
+                out=sorted_.rearrange("k (t p) -> k p t", t=PACK),
+                in_=plain.rearrange("k (p t) -> k p t", t=PACK),
             )
-            rows = work.tile([P, K_PASS], BF16, tag="cq_rows%d" % a, name="cq_rows%d_%d" % (g, a))
-            nc.scalar.copy(
-                out=rows[:].rearrange("r (u p e) -> r u p e", u=2, e=2),
-                in_=cq_bank[:].rearrange("r (p u e) -> r u p e", u=2, e=2),
-            )
-            cq_rows[(g, a)] = rows
 
-        def flip(g):
-            flipped = bank(6 + g % STEP_GROUPS, "cq_flipped%d" % g)
-            for a in range(TOKEN_TILES):
-                pairs = cq_rows[(g, a)][:].bitcast(F32)
-                for u in range(2):
-                    nc.tensor.transpose(
-                        flipped[:, (2 * a + u) * P : (2 * a + u + 1) * P],
-                        pairs[:, u * P : (u + 1) * P],
-                        identity[:],
-                    )
-            grouped = work.tile(
-                [P, TOKENS * PACK], BF16, tag="cq_grouped", name="cq_grouped%d" % g, align_bytes=64
+        def sort_group(g):
+            plane, place = divmod(g, PLANE_GROUPS)
+            cols = slice(place * K_PASS, (place + 1) * K_PASS)
+            if plane == 0:
+                sort_columns(wqa_sorted_planes[:, cols], wqa_planes[:, cols])
+            words = work.tile([P, K_PASS], I32, tag="sorted", name="sorted%d" % g, align_bytes=64)
+            sort_columns(words[:], wqa_words[g][:].bitcast(I32))
+            sorted_words[g] = words
+
+        def project(turn, a):
+            g = ORDER[turn]
+            plane, place = divmod(g, PLANE_GROUPS)
+            if a == 0:
+                cq_grouped[g] = work.tile(
+                    [P, TOKENS * PACK], BF16, tag="cq_grouped", name="cq_grouped%d" % g, align_bytes=64
+                )
+            cq_bank = bank(4 + 2 * (turn % 2) + a, "cq_bank%d_%d" % (g, a))
+            for t in range(PACK):
+                first = place * K_PASS + t * P
+                nc.tensor.matmul_mx(
+                    out=cq_bank[:, t * P : (t + 1) * P],
+                    lhsT=sorted_words[g][:, t * P : (t + 1) * P].bitcast(FP8X4),
+                    lhsT_scale=wqa_sorted_planes[4 * plane : P, first : first + P],
+                    rhs=x_codes[:, a * P : (a + 1) * P].bitcast(FP8X4),
+                    rhs_scale=x_scales[:, a * P : (a + 1) * P],
+                    start=True,
+                    stop=True,
+                )
+            nc.scalar.copy(
+                out=cq_grouped[g][:, a * K_PASS : (a + 1) * K_PASS].rearrange(
+                    "p (r t) -> p r t", t=PACK
+                ),
+                in_=cq_bank[:].rearrange("p (t r) -> p r t", t=PACK),
             )
-            regroup(grouped[:], flipped[:])
-            cq_grouped[g] = grouped
 
         def pack(g):
             codes = keep.tile([P, TOKENS], U32, name="cq_codes%d" % g, align_bytes=64)
@@ -210,15 +218,15 @@ def tile_multilatentattention_pa_k_kernel(
 
         def accumulate(acc, g, a, chunk):
             codes, scales = cq_codes[g]
-            s, plane = divmod(g, PLANES_PER_TILE)
+            plane, s = divmod(g, PLANE_GROUPS)
             nc.tensor.matmul_mx(
                 out=acc[:],
                 lhsT=codes[:, a * P : (a + 1) * P].bitcast(FP8X4),
                 lhsT_scale=scales[:, a * P : (a + 1) * P],
                 rhs=wqb_words[(g, chunk)].bitcast(FP8X4),
                 rhs_scale=wqb_planes[s][4 * plane : P, chunk * BANK_COLS : (chunk + 1) * BANK_COLS],
-                start=(g == 0),
-                stop=(g == GROUPS - 1),
+                start=(g == ORDER[0]),
+                stop=(g == ORDER[-1]),
             )
 
         def open_round(half, first_bank):
@@ -230,23 +238,19 @@ def tile_multilatentattention_pa_k_kernel(
 
         first_round = open_round(0, 0)
 
-        def advance(g):
+        sort_group(ORDER[0])
+        for turn in range(GROUPS + LAG):
+            if turn + 1 < GROUPS:
+                sort_group(ORDER[turn + 1])
             for a in range(TOKEN_TILES):
-                if g < GROUPS:
-                    project(g, a)
-                if g >= LAG:
+                if turn < GROUPS:
+                    project(turn, a)
+                if turn >= LAG:
                     for acc, acc_tile, chunk in first_round:
                         if acc_tile == a:
-                            accumulate(acc, g - LAG, a, chunk)
-
-        for first in range(0, GROUPS + LAG, STEP_GROUPS):
-            advance(first)
-            made_before = [g for g in range(first - STEP_GROUPS, first) if 0 <= g < GROUPS]
-            for g in made_before:
-                flip(g)
-            for g in made_before:
-                pack(g)
-            advance(first + 1)
+                            accumulate(acc, ORDER[turn - LAG], a, chunk)
+            if turn < GROUPS:
+                pack(ORDER[turn])
 
         position_int = keep.tile([P, 1], I32)
         nc.vector.tensor_single_scalar(
@@ -329,10 +333,10 @@ def tile_multilatentattention_pa_k_kernel(
             finish(acc, a, chunk)
 
         second_round = open_round(1, 4)
-        for g in range(GROUPS - TAIL_GROUPS):
+        for g in ORDER[:-TAIL_GROUPS]:
             for acc, a, chunk in second_round:
                 accumulate(acc, g, a, chunk)
         for acc, a, chunk in second_round:
-            for g in range(GROUPS - TAIL_GROUPS, GROUPS):
+            for g in ORDER[-TAIL_GROUPS:]:
                 accumulate(acc, g, a, chunk)
             finish(acc, a, chunk)

@@ -20,6 +20,7 @@ BANK_COLS = 512
 
 BATCH, POSITIONS, FEATURES = 4, 64, 512
 TOKEN_TILES = BATCH * POSITIONS // P
+BATCHES_PER_TILE = BATCH // TOKEN_TILES
 TOKENS = TOKEN_TILES * P
 INNER = 8192
 GROUPS = INNER // K_PASS
@@ -50,7 +51,8 @@ def tile_multilatentattention_pa_k_kernel(
     with ExitStack() as stack:
         keep = stack.enter_context(tc.tile_pool(name="keep", bufs=1))
         work = stack.enter_context(tc.tile_pool(name="work", bufs=4))
-        results = stack.enter_context(tc.tile_pool(name="results", bufs=4))
+        results = stack.enter_context(tc.tile_pool(name="results", bufs=8))
+        products = stack.enter_context(tc.tile_pool(name="products", bufs=2))
         psum = stack.enter_context(tc.psum_pool(name="psum", bufs=1))
         stack.enter_context(tc.manual_schedule())
 
@@ -296,15 +298,15 @@ def tile_multilatentattention_pa_k_kernel(
             out=for_odd[:, 1, :], in_=part_turn[:, COS, :], func=ACT.Sin, scale=2.0 * math.pi
         )
 
-        def finish(acc, a, chunk):
+        def finish(acc, a, chunk, queue):
             label = "%d_%d" % (a, chunk)
             summed = acc[:].rearrange("r (h d) -> r h d", h=HEADS_PER_BANK)
             heads = results.tile([P, HEADS_PER_BANK, HEAD_DIM], F32, tag="heads", name="heads" + label)
             nc.scalar.copy(out=heads[:, :, 0:NOPE], in_=summed[:, :, 0:NOPE])
             pairs = summed[:, :, NOPE:HEAD_DIM].rearrange("r h (i e) -> r h i e", e=2)
             shape = [P, HEADS_PER_BANK, 2, PAIRS]
-            from_even = results.tile(shape, F32, tag="from_even", name="from_even" + label)
-            from_odd = results.tile(shape, F32, tag="from_odd", name="from_odd" + label)
+            from_even = products.tile(shape, F32, tag="from_even", name="from_even" + label)
+            from_odd = products.tile(shape, F32, tag="from_odd", name="from_odd" + label)
             nc.vector.tensor_tensor(
                 out=from_even[:],
                 in0=pairs[:, :, :, 0].unsqueeze(2).to_broadcast(shape),
@@ -323,14 +325,16 @@ def tile_multilatentattention_pa_k_kernel(
                 in1=from_odd[:].rearrange("r h e i -> r h i e"),
                 op=ALU.add,
             )
-            for h in range(HEADS_PER_BANK):
-                nc.sync.dma_start(
-                    out=out[2 * a : 2 * a + 2, HEADS_PER_BANK * chunk + h].rearrange("b n d -> n b d"),
-                    in_=heads[:, h, :],
+            for b in range(BATCHES_PER_TILE):
+                queue.dma_start(
+                    out=out[
+                        BATCHES_PER_TILE * a + b, HEADS_PER_BANK * chunk : HEADS_PER_BANK * (chunk + 1)
+                    ].rearrange("h n d -> n h d"),
+                    in_=heads[b:P:BATCHES_PER_TILE, :, :],
                 )
 
         for acc, a, chunk in first_round:
-            finish(acc, a, chunk)
+            finish(acc, a, chunk, nc.gpsimd)
 
         second_round = open_round(1, 4)
         for g in ORDER[:-TAIL_GROUPS]:
@@ -339,4 +343,4 @@ def tile_multilatentattention_pa_k_kernel(
         for acc, a, chunk in second_round:
             for g in ORDER[-TAIL_GROUPS:]:
                 accumulate(acc, g, a, chunk)
-            finish(acc, a, chunk)
+            finish(acc, a, chunk, nc.sync)

@@ -34,7 +34,7 @@ CHUNKS_PER_HALF = HALF_COLS // BANK_COLS
 
 PLANES_PER_TILE = 4
 QUADRANTS = 4
-LAG = 4
+LAG = 3
 PLANE_GROUPS = GROUPS // PLANES_PER_TILE
 ORDER = [place + PLANE_GROUPS * plane for place in range(PLANE_GROUPS) for plane in range(PLANES_PER_TILE)]
 TAIL_GROUPS = 4
@@ -63,10 +63,10 @@ def tile_multilatentattention_pa_k_kernel(
         nc.vector.memset(wqa_planes[:].bitcast(I32), 0)
         wqa_sorted_planes = keep.tile([P, INNER // PLANES_PER_TILE], U8, align_bytes=64)
         wqb_planes = []
-        for s in range(GROUPS // PLANES_PER_TILE):
+        for s in range(PLANE_GROUPS):
             planes = keep.tile([P, Q_COLS], U8, name="wqb_planes%d" % s, align_bytes=64)
-            nc.vector.memset(planes[:].bitcast(I32), 0)
             wqb_planes.append(planes)
+        nc.vector.memset(wqb_planes[0][:].bitcast(I32), 0)
 
         identity = keep.tile([P, P], F32)
         make_identity(nc, identity[:])
@@ -76,32 +76,14 @@ def tile_multilatentattention_pa_k_kernel(
         wqa_words_dram = Wqa_words[0].rearrange("p n t -> p (n t)").bitcast(I32)
         wqa_scales_dram = Wqa_scales[0].bitcast(I32)
         wqb_words_dram = Wqb_words.rearrange("g p n t -> g p (n t)").bitcast(I32)
-        wqb_scales_dram = Wqb_scales.bitcast(F32)
 
         x_rows = []
         for a in range(TOKEN_TILES):
             rows = keep.tile([P, FEATURES], BF16, name="x_rows%d" % a)
-            nc.sync.dma_start(out=rows[:], in_=x[2 * a : 2 * a + 2].rearrange("b n e -> n b e"))
             x_rows.append(rows)
 
-        for quadrant in range(QUADRANTS):
-            nc.sync.dma_start(
-                out=wqa_planes[32 * quadrant : 32 * quadrant + 16, :].bitcast(I32),
-                in_=wqa_scales_dram[4 * quadrant : 4 * quadrant + 4, :].rearrange(
-                    "r (i n) -> i r n", i=PLANES_PER_TILE
-                ),
-            )
-
-        for s in range(GROUPS // PLANES_PER_TILE):
-            for quadrant in range(QUADRANTS):
-                nc.gpsimd.dma_start(
-                    out=wqb_planes[s][32 * quadrant : 32 * quadrant + 16, :].bitcast(F32),
-                    in_=wqb_scales_dram[
-                        s : GROUPS : PLANE_GROUPS,
-                        4 * quadrant : 4 * quadrant + 4,
-                        :,
-                    ],
-                )
+        def load_x(a):
+            nc.sync.dma_start(out=x_rows[a][:], in_=x[2 * a : 2 * a + 2].rearrange("b n e -> n b e"))
 
         wqa_words = {}
 
@@ -113,7 +95,30 @@ def tile_multilatentattention_pa_k_kernel(
             )
             wqa_words[g] = words
 
-        for turn in range(LAG):
+        load_x(0)
+        load_wqa_group()
+        load_x(1)
+
+        for quadrant in range(QUADRANTS):
+            nc.sync.dma_start(
+                out=wqa_planes[32 * quadrant : 32 * quadrant + 16, :].bitcast(I32),
+                in_=wqa_scales_dram[4 * quadrant : 4 * quadrant + 4, :].rearrange(
+                    "r (i n) -> i r n", i=PLANES_PER_TILE
+                ),
+            )
+
+        def load_wqb_planes(s, queue, dtype):
+            for quadrant in range(QUADRANTS):
+                queue.dma_start(
+                    out=wqb_planes[s][32 * quadrant : 32 * quadrant + 16, :].bitcast(dtype),
+                    in_=Wqb_scales.bitcast(dtype)[
+                        s : GROUPS : PLANE_GROUPS, 4 * quadrant : 4 * quadrant + 4, :
+                    ],
+                )
+
+        load_wqb_planes(0, nc.sync, I32)
+
+        for turn in range(1, LAG):
             load_wqa_group()
         wqb_words = {}
 
@@ -148,6 +153,13 @@ def tile_multilatentattention_pa_k_kernel(
                 in_=flipped.rearrange("p (a u r) -> p a r u", r=P, u=2),
             )
 
+        def quantise_x(a):
+            nc.vector.quantize_mx(
+                out=x_codes[:, a * P : (a + 1) * P].bitcast(FP8X4),
+                scales=x_scales[:, a * P : (a + 1) * P],
+                in_=x_grouped[:, a * K_PASS : (a + 1) * K_PASS],
+            )
+
         x_grouped = keep.tile([P, TOKENS * PACK], BF16, align_bytes=64)
         x_codes = keep.tile([P, TOKENS], U32, align_bytes=64)
         x_scales = keep.tile([P, TOKENS], U8, align_bytes=64)
@@ -159,29 +171,29 @@ def tile_multilatentattention_pa_k_kernel(
                     x_flipped[:, u * P : (u + 1) * P], x_pairs[:, u : FEATURES // 2 : 2], identity[:]
                 )
             regroup(x_grouped[:, a * K_PASS : (a + 1) * K_PASS], x_flipped[:, 0 : 2 * P])
-            nc.vector.quantize_mx(
-                out=x_codes[:, a * P : (a + 1) * P].bitcast(FP8X4),
-                scales=x_scales[:, a * P : (a + 1) * P],
-                in_=x_grouped[:, a * K_PASS : (a + 1) * K_PASS],
-            )
+        for a in range(TOKEN_TILES):
+            quantise_x(a)
 
         sorted_words = {}
         cq_grouped = {}
         cq_codes = {}
 
-        def sort_columns(sorted_, plain):
+        def sort_words(sorted_, plain):
             nc.vector.tensor_copy(
-                out=sorted_.rearrange("k (t p) -> k p t", t=PACK),
-                in_=plain.rearrange("k (p t) -> k p t", t=PACK),
+                out=sorted_.rearrange("k (t c i) -> k c t i", t=PACK, i=PACK),
+                in_=plain.rearrange("k (c i t) -> k c t i", t=PACK, i=PACK),
+            )
+
+        def sort_scales(place):
+            cols = slice(place * K_PASS, (place + 1) * K_PASS)
+            nc.vector.tensor_copy(
+                out=wqa_sorted_planes[:, cols].rearrange("k (t p) -> k p t", t=PACK),
+                in_=wqa_planes[:, cols].rearrange("k (p t) -> k p t", t=PACK),
             )
 
         def sort_group(g):
-            plane, place = divmod(g, PLANE_GROUPS)
-            cols = slice(place * K_PASS, (place + 1) * K_PASS)
-            if plane == 0:
-                sort_columns(wqa_sorted_planes[:, cols], wqa_planes[:, cols])
             words = work.tile([P, K_PASS], I32, tag="sorted", name="sorted%d" % g, align_bytes=64)
-            sort_columns(words[:], wqa_words[g][:].bitcast(I32))
+            sort_words(words[:], wqa_words[g][:].bitcast(I32))
             sorted_words[g] = words
 
         def project(turn, a):
@@ -241,9 +253,13 @@ def tile_multilatentattention_pa_k_kernel(
         first_round = open_round(0, 0)
 
         sort_group(ORDER[0])
+        sort_scales(0)
         for turn in range(GROUPS + LAG):
             if turn + 1 < GROUPS:
                 sort_group(ORDER[turn + 1])
+            if turn + 1 < PLANE_GROUPS:
+                nc.vector.memset(wqb_planes[turn + 1][:].bitcast(I32), 0)
+                load_wqb_planes(turn + 1, nc.gpsimd, F32)
             for a in range(TOKEN_TILES):
                 if turn < GROUPS:
                     project(turn, a)
@@ -253,6 +269,8 @@ def tile_multilatentattention_pa_k_kernel(
                             accumulate(acc, ORDER[turn - LAG], a, chunk)
             if turn < GROUPS:
                 pack(ORDER[turn])
+            if 1 <= turn < PLANE_GROUPS:
+                sort_scales(turn)
 
         position_int = keep.tile([P, 1], I32)
         nc.vector.tensor_single_scalar(

@@ -316,7 +316,7 @@ def tile_multilatentattention_pa_k_kernel(
             out=for_odd[:, 1, :], in_=part_turn[:, COS, :], func=ACT.Sin, scale=2.0 * math.pi
         )
 
-        def finish(acc, a, chunk, queue):
+        def finish(acc, a, chunk):
             label = "%d_%d" % (a, chunk)
             summed = acc[:].rearrange("r (h d) -> r h d", h=HEADS_PER_BANK)
             heads = results.tile([P, HEADS_PER_BANK, HEAD_DIM], F32, tag="heads", name="heads" + label)
@@ -344,7 +344,7 @@ def tile_multilatentattention_pa_k_kernel(
                 op=ALU.add,
             )
             for b in range(BATCHES_PER_TILE):
-                queue.dma_start(
+                nc.sync.dma_start(
                     out=out[
                         BATCHES_PER_TILE * a + b, HEADS_PER_BANK * chunk : HEADS_PER_BANK * (chunk + 1)
                     ].rearrange("h n d -> n h d"),
@@ -352,7 +352,7 @@ def tile_multilatentattention_pa_k_kernel(
                 )
 
         for acc, a, chunk in first_round:
-            finish(acc, a, chunk, nc.gpsimd)
+            finish(acc, a, chunk)
 
         second_round = open_round(1, 4)
         for g in ORDER[:-TAIL_GROUPS]:
@@ -361,4 +361,4 @@ def tile_multilatentattention_pa_k_kernel(
         for acc, a, chunk in second_round:
             for g in ORDER[-TAIL_GROUPS:]:
                 accumulate(acc, g, a, chunk)
-            finish(acc, a, chunk, nc.sync)
+            finish(acc, a, chunk)

import math
from contextlib import ExitStack

import concourse.mybir as mybir
from concourse.masks import make_identity

F32 = mybir.dt.float32
BF16 = mybir.dt.bfloat16
I32 = mybir.dt.int32
U32 = mybir.dt.uint32
U8 = mybir.dt.uint8
FP8X4 = mybir.dt.float8_e4m3fn_x4
ALU = mybir.AluOpType
ACT = mybir.ActivationFunctionType

P = 128
PACK = 4
K_PASS = P * PACK
BANK_COLS = 512

BATCH, POSITIONS, FEATURES = 4, 64, 512
TOKEN_TILES = BATCH * POSITIONS // P
BATCHES_PER_TILE = BATCH // TOKEN_TILES
TOKENS = TOKEN_TILES * P
INNER = 8192
GROUPS = INNER // K_PASS
HEADS, HEAD_DIM, NOPE = 16, 128, 64
PAIRS = (HEAD_DIM - NOPE) // 2
ROPE_BASE = 10000.0
Q_COLS = HEADS * HEAD_DIM
HEADS_PER_BANK = BANK_COLS // HEAD_DIM
HALF_COLS = Q_COLS // 2
CHUNKS_PER_HALF = HALF_COLS // BANK_COLS

PLANES_PER_TILE = 4
QUADRANTS = 4
LAG = 3
PLANE_GROUPS = GROUPS // PLANES_PER_TILE
ORDER = [place + PLANE_GROUPS * plane for place in range(PLANE_GROUPS) for plane in range(PLANES_PER_TILE)]
TAIL_GROUPS = 4

ROUND_TO_WHOLE = 1.5 * 2.0**23

FLOPS = 2 * TOKENS * FEATURES * INNER + 2 * TOKENS * INNER * Q_COLS


def tile_multilatentattention_pa_k_kernel(
    tc, x, Wqa_words, Wqa_scales, Wqb_words, Wqb_scales, out
):
    nc = tc.nc
    with ExitStack() as stack:
        keep = stack.enter_context(tc.tile_pool(name="keep", bufs=1))
        work = stack.enter_context(tc.tile_pool(name="work", bufs=4))
        results = stack.enter_context(tc.tile_pool(name="results", bufs=8))
        products = stack.enter_context(tc.tile_pool(name="products", bufs=2))
        psum = stack.enter_context(tc.psum_pool(name="psum", bufs=1))
        stack.enter_context(tc.manual_schedule())

        def bank(index, name):
            return psum.tile([P, BANK_COLS], F32, tag="bank%d" % index, name=name)

        wqa_planes = keep.tile([P, INNER // PLANES_PER_TILE], U8, align_bytes=64)
        nc.vector.memset(wqa_planes[:].bitcast(I32), 0)
        wqa_sorted_planes = keep.tile([P, INNER // PLANES_PER_TILE], U8, align_bytes=64)
        wqb_planes = []
        for s in range(PLANE_GROUPS):
            planes = keep.tile([P, Q_COLS], U8, name="wqb_planes%d" % s, align_bytes=64)
            wqb_planes.append(planes)
        nc.vector.memset(wqb_planes[0][:].bitcast(I32), 0)

        identity = keep.tile([P, P], F32)
        make_identity(nc, identity[:])
        partition_index = keep.tile([P, 1], I32)
        nc.gpsimd.iota(partition_index[:], pattern=[[0, 1]], base=0, channel_multiplier=1)

        wqa_words_dram = Wqa_words[0].rearrange("p n t -> p (n t)").bitcast(I32)
        wqa_scales_dram = Wqa_scales[0].bitcast(I32)
        wqb_words_dram = Wqb_words.rearrange("g p n t -> g p (n t)").bitcast(I32)

        x_rows = []
        for a in range(TOKEN_TILES):
            rows = keep.tile([P, FEATURES], BF16, name="x_rows%d" % a)
            x_rows.append(rows)

        def load_x(a):
            nc.sync.dma_start(out=x_rows[a][:], in_=x[2 * a : 2 * a + 2].rearrange("b n e -> n b e"))

        wqa_words = {}

        def load_wqa_group():
            g = ORDER[len(wqa_words)]
            words = keep.tile([P, K_PASS], U32, name="wqa_words%d" % g, align_bytes=64)
            nc.sync.dma_start(
                out=words[:].bitcast(I32), in_=wqa_words_dram[:, g * K_PASS : (g + 1) * K_PASS]
            )
            wqa_words[g] = words

        load_x(0)
        load_wqa_group()
        load_x(1)

        for quadrant in range(QUADRANTS):
            nc.sync.dma_start(
                out=wqa_planes[32 * quadrant : 32 * quadrant + 16, :].bitcast(I32),
                in_=wqa_scales_dram[4 * quadrant : 4 * quadrant + 4, :].rearrange(
                    "r (i n) -> i r n", i=PLANES_PER_TILE
                ),
            )

        def load_wqb_planes(s, queue, dtype):
            for quadrant in range(QUADRANTS):
                queue.dma_start(
                    out=wqb_planes[s][32 * quadrant : 32 * quadrant + 16, :].bitcast(dtype),
                    in_=Wqb_scales.bitcast(dtype)[
                        s : GROUPS : PLANE_GROUPS, 4 * quadrant : 4 * quadrant + 4, :
                    ],
                )

        load_wqb_planes(0, nc.sync, I32)

        for turn in range(1, LAG):
            load_wqa_group()
        wqb_words = {}

        def load_wqb(g, first_chunk, chunks):
            words = keep.tile(
                [P, chunks * BANK_COLS], U32, name="wqb_words%d_%d" % (g, first_chunk), align_bytes=64
            )
            nc.sync.dma_start(
                out=words[:].bitcast(I32),
                in_=wqb_words_dram[
                    g, :, first_chunk * BANK_COLS : (first_chunk + chunks) * BANK_COLS
                ],
            )
            for place in range(chunks):
                wqb_words[(g, first_chunk + place)] = words[
                    :, place * BANK_COLS : (place + 1) * BANK_COLS
                ]

        for g in ORDER:
            load_wqb(g, 0, CHUNKS_PER_HALF)
            if len(wqa_words) < GROUPS:
                load_wqa_group()
        for g in ORDER[:-TAIL_GROUPS]:
            load_wqb(g, CHUNKS_PER_HALF, CHUNKS_PER_HALF)
        for chunk in range(CHUNKS_PER_HALF, 2 * CHUNKS_PER_HALF):
            for g in ORDER[-TAIL_GROUPS:]:
                load_wqb(g, chunk, 1)

        def regroup(grouped, flipped):
            nc.vector.tensor_copy(
                out=grouped.bitcast(F32).rearrange("p (a r u) -> p a r u", r=P, u=2),
                in_=flipped.rearrange("p (a u r) -> p a r u", r=P, u=2),
            )

        def quantise_x(a):
            nc.vector.quantize_mx(
                out=x_codes[:, a * P : (a + 1) * P].bitcast(FP8X4),
                scales=x_scales[:, a * P : (a + 1) * P],
                in_=x_grouped[:, a * K_PASS : (a + 1) * K_PASS],
            )

        x_grouped = keep.tile([P, TOKENS * PACK], BF16, align_bytes=64)
        x_codes = keep.tile([P, TOKENS], U32, align_bytes=64)
        x_scales = keep.tile([P, TOKENS], U8, align_bytes=64)
        for a in range(TOKEN_TILES):
            x_flipped = bank(6 + a, "x_flipped%d" % a)
            x_pairs = x_rows[a][:].bitcast(F32)
            for u in range(2):
                nc.tensor.transpose(
                    x_flipped[:, u * P : (u + 1) * P], x_pairs[:, u : FEATURES // 2 : 2], identity[:]
                )
            regroup(x_grouped[:, a * K_PASS : (a + 1) * K_PASS], x_flipped[:, 0 : 2 * P])
        for a in range(TOKEN_TILES):
            quantise_x(a)

        sorted_words = {}
        cq_grouped = {}
        cq_codes = {}

        def sort_words(sorted_, plain):
            nc.vector.tensor_copy(
                out=sorted_.rearrange("k (t c i) -> k c t i", t=PACK, i=PACK),
                in_=plain.rearrange("k (c i t) -> k c t i", t=PACK, i=PACK),
            )

        def sort_scales(place):
            cols = slice(place * K_PASS, (place + 1) * K_PASS)
            nc.vector.tensor_copy(
                out=wqa_sorted_planes[:, cols].rearrange("k (t p) -> k p t", t=PACK),
                in_=wqa_planes[:, cols].rearrange("k (p t) -> k p t", t=PACK),
            )

        def sort_group(g):
            words = work.tile([P, K_PASS], I32, tag="sorted", name="sorted%d" % g, align_bytes=64)
            sort_words(words[:], wqa_words[g][:].bitcast(I32))
            sorted_words[g] = words

        def project(turn, a):
            g = ORDER[turn]
            plane, place = divmod(g, PLANE_GROUPS)
            if a == 0:
                cq_grouped[g] = work.tile(
                    [P, TOKENS * PACK], BF16, tag="cq_grouped", name="cq_grouped%d" % g, align_bytes=64
                )
            cq_bank = bank(4 + 2 * (turn % 2) + a, "cq_bank%d_%d" % (g, a))
            for t in range(PACK):
                first = place * K_PASS + t * P
                nc.tensor.matmul_mx(
                    out=cq_bank[:, t * P : (t + 1) * P],
                    lhsT=sorted_words[g][:, t * P : (t + 1) * P].bitcast(FP8X4),
                    lhsT_scale=wqa_sorted_planes[4 * plane : P, first : first + P],
                    rhs=x_codes[:, a * P : (a + 1) * P].bitcast(FP8X4),
                    rhs_scale=x_scales[:, a * P : (a + 1) * P],
                    start=True,
                    stop=True,
                )
            nc.scalar.copy(
                out=cq_grouped[g][:, a * K_PASS : (a + 1) * K_PASS].rearrange(
                    "p (r t) -> p r t", t=PACK
                ),
                in_=cq_bank[:].rearrange("p (t r) -> p r t", t=PACK),
            )

        def pack(g):
            codes = keep.tile([P, TOKENS], U32, name="cq_codes%d" % g, align_bytes=64)
            scales = keep.tile([P, TOKENS], U8, name="cq_scales%d" % g, align_bytes=64)
            nc.vector.quantize_mx(
                out=codes[:].bitcast(FP8X4), scales=scales[:], in_=cq_grouped[g][:]
            )
            cq_codes[g] = (codes, scales)

        def accumulate(acc, g, a, chunk):
            codes, scales = cq_codes[g]
            plane, s = divmod(g, PLANE_GROUPS)
            nc.tensor.matmul_mx(
                out=acc[:],
                lhsT=codes[:, a * P : (a + 1) * P].bitcast(FP8X4),
                lhsT_scale=scales[:, a * P : (a + 1) * P],
                rhs=wqb_words[(g, chunk)].bitcast(FP8X4),
                rhs_scale=wqb_planes[s][4 * plane : P, chunk * BANK_COLS : (chunk + 1) * BANK_COLS],
                start=(g == ORDER[0]),
                stop=(g == ORDER[-1]),
            )

        def open_round(half, first_bank):
            accs = []
            for chunk in range(half * CHUNKS_PER_HALF, (half + 1) * CHUNKS_PER_HALF):
                for a in range(TOKEN_TILES):
                    accs.append((bank(first_bank + len(accs), "acc%d_%d" % (a, chunk)), a, chunk))
            return accs

        first_round = open_round(0, 0)

        sort_group(ORDER[0])
        sort_scales(0)
        for turn in range(GROUPS + LAG):
            if turn + 1 < GROUPS:
                sort_group(ORDER[turn + 1])
            if turn + 1 < PLANE_GROUPS:
                nc.vector.memset(wqb_planes[turn + 1][:].bitcast(I32), 0)
                load_wqb_planes(turn + 1, nc.gpsimd, F32)
            for a in range(TOKEN_TILES):
                if turn < GROUPS:
                    project(turn, a)
                if turn >= LAG:
                    for acc, acc_tile, chunk in first_round:
                        if acc_tile == a:
                            accumulate(acc, ORDER[turn - LAG], a, chunk)
            if turn < GROUPS:
                pack(ORDER[turn])
            if 1 <= turn < PLANE_GROUPS:
                sort_scales(turn)

        position_int = keep.tile([P, 1], I32)
        nc.vector.tensor_single_scalar(
            out=position_int[:], in_=partition_index[:], scalar=1, op=ALU.arith_shift_right
        )
        position = keep.tile([P, 1], F32)
        nc.vector.tensor_copy(out=position[:], in_=position_int[:])
        turns = keep.tile([P, PAIRS], F32)
        nc.vector.tensor_single_scalar(
            out=turns[:, 0:1], in_=position[:], scalar=1.0 / (2.0 * math.pi), op=ALU.mult
        )
        width = 1
        while width < PAIRS:
            nc.vector.tensor_single_scalar(
                out=turns[:, width : 2 * width],
                in_=turns[:, 0:width],
                scalar=ROPE_BASE ** (-width / PAIRS),
                op=ALU.mult,
            )
            width *= 2
        COS, SIN = 0, 1
        shifted = keep.tile([P, 2, PAIRS], F32)
        nc.vector.tensor_single_scalar(out=shifted[:, COS, :], in_=turns[:], scalar=0.25, op=ALU.add)
        nc.vector.tensor_copy(out=shifted[:, SIN, :], in_=turns[:])
        whole = keep.tile([P, 2, PAIRS], F32)
        nc.vector.tensor_scalar(
            out=whole[:],
            in0=shifted[:],
            scalar1=ROUND_TO_WHOLE,
            scalar2=ROUND_TO_WHOLE,
            op0=ALU.add,
            op1=ALU.subtract,
        )
        part_turn = keep.tile([P, 2, PAIRS], F32)
        nc.vector.tensor_tensor(out=part_turn[:], in0=shifted[:], in1=whole[:], op=ALU.subtract)
        for_even = keep.tile([P, 2, PAIRS], F32)
        for_odd = keep.tile([P, 2, PAIRS], F32)
        nc.scalar.activation(out=for_even[:], in_=part_turn[:], func=ACT.Sin, scale=2.0 * math.pi)
        nc.scalar.activation(
            out=for_odd[:, 0, :], in_=part_turn[:, SIN, :], func=ACT.Sin, scale=-2.0 * math.pi
        )
        nc.scalar.activation(
            out=for_odd[:, 1, :], in_=part_turn[:, COS, :], func=ACT.Sin, scale=2.0 * math.pi
        )

        def finish(acc, a, chunk):
            label = "%d_%d" % (a, chunk)
            summed = acc[:].rearrange("r (h d) -> r h d", h=HEADS_PER_BANK)
            heads = results.tile([P, HEADS_PER_BANK, HEAD_DIM], F32, tag="heads", name="heads" + label)
            nc.scalar.copy(out=heads[:, :, 0:NOPE], in_=summed[:, :, 0:NOPE])
            pairs = summed[:, :, NOPE:HEAD_DIM].rearrange("r h (i e) -> r h i e", e=2)
            shape = [P, HEADS_PER_BANK, 2, PAIRS]
            from_even = products.tile(shape, F32, tag="from_even", name="from_even" + label)
            from_odd = products.tile(shape, F32, tag="from_odd", name="from_odd" + label)
            nc.vector.tensor_tensor(
                out=from_even[:],
                in0=pairs[:, :, :, 0].unsqueeze(2).to_broadcast(shape),
                in1=for_even[:].unsqueeze(1).to_broadcast(shape),
                op=ALU.mult,
            )
            nc.vector.tensor_tensor(
                out=from_odd[:],
                in0=pairs[:, :, :, 1].unsqueeze(2).to_broadcast(shape),
                in1=for_odd[:].unsqueeze(1).to_broadcast(shape),
                op=ALU.mult,
            )
            nc.vector.tensor_tensor(
                out=heads[:, :, NOPE:HEAD_DIM].rearrange("r h (i e) -> r h i e", e=2),
                in0=from_even[:].rearrange("r h e i -> r h i e"),
                in1=from_odd[:].rearrange("r h e i -> r h i e"),
                op=ALU.add,
            )
            for b in range(BATCHES_PER_TILE):
                nc.sync.dma_start(
                    out=out[
                        BATCHES_PER_TILE * a + b, HEADS_PER_BANK * chunk : HEADS_PER_BANK * (chunk + 1)
                    ].rearrange("h n d -> n h d"),
                    in_=heads[b:P:BATCHES_PER_TILE, :, :],
                )

        for acc, a, chunk in first_round:
            finish(acc, a, chunk)

        second_round = open_round(1, 4)
        for g in ORDER[:-TAIL_GROUPS]:
            for acc, a, chunk in second_round:
                accumulate(acc, g, a, chunk)
        for acc, a, chunk in second_round:
            for g in ORDER[-TAIL_GROUPS:]:
                accumulate(acc, g, a, chunk)
            finish(acc, a, chunk)
